import numpy as np
import ml_dtypes


def mxq(x, axis, fmt="e4m3"):
    dtype, down = {"e4m3": (ml_dtypes.float8_e4m3fn, 7), "e5m2": (ml_dtypes.float8_e5m2, 14)}[fmt]
    v = np.moveaxis(np.asarray(x, np.float32).astype(ml_dtypes.bfloat16).astype(np.float64), axis, -1)
    blocks = v.reshape(v.shape[:-1] + (-1, 32))
    amax = np.abs(blocks).max(-1, keepdims=True)
    byte = np.maximum(np.where(amax > 0, np.frexp(amax)[1] - 1 + 127, 0) - down, 1)
    scale = np.exp2(byte - 127.0)
    codes = (blocks / scale).astype(np.float32).astype(dtype).astype(np.float64)
    return np.moveaxis((codes * scale).reshape(v.shape), -1, axis)


WIDE = False


def mx_kscale(k):
    if not WIDE:
        return np.ones(k)
    levels = np.array([10, -10, 5, -5, 0])
    if k % 512:
        return np.exp2(np.random.permutation(np.resize(levels, k // 32))).repeat(32)
    a = np.empty((k // 512, 16))
    for p in range(k // 512):
        a[p, :8] = np.random.permutation(np.resize(levels, 8))
        for g in range(8):
            far = levels[np.abs(levels - a[p, g]) >= 10]
            a[p, g + 8] = far[np.random.randint(len(far))]
    return np.exp2(a.ravel()).repeat(32)


BF16 = ml_dtypes.bfloat16


def bf(x):
    return np.asarray(x, np.float32).astype(BF16)


def f64(x):
    return np.asarray(x).astype(np.float64)


B, T, G, I, H = 2, 64, 8, 512, 256


def setup_inputs():
    s = mx_kscale(I)
    return {"x": bf((np.random.standard_normal((B, T, G, I)) * s).reshape(B, T, G * I)),
            "W": bf(np.random.standard_normal((G, H, I)) / np.sqrt(I) / s),
            "b": bf(np.random.standard_normal((G, H)) * 0.5)}


def reference(x, W, b):
    xg = f64(x).reshape(B, T, G, I)
    xq = mxq(xg, 3, "e4m3")
    wq = mxq(f64(W), 2, "e4m3")
    y = xq.transpose(2, 0, 1, 3).reshape(G, B * T, I) @ wq.transpose(0, 2, 1)
    out = y.reshape(G, B, T, H).transpose(1, 2, 0, 3) + f64(b)
    return np.swapaxes(out, -1, -2).reshape(B, T, G * H)

@@ -1,0 +1,144 @@
+import concourse.mybir as mybir
+from concourse.masks import make_identity
+
+F32 = mybir.dt.float32
+BF16 = mybir.dt.bfloat16
+U32 = mybir.dt.uint32
+U8 = mybir.dt.uint8
+FP8X4 = mybir.dt.float8_e4m3fn_x4
+
+P = 128
+G = 8
+I = 512
+H = 256
+QUAD = 4
+B_ROWS = G * H // P
+
+FLOPS = 2 * P * G * I * H
+
+
+def tile_groupedlinear_s_kernel(tc, x, W, b, out):
+    nc = tc.nc
+    x_rows = x.flatten_outer_dims()
+    out_rows = out.flatten_outer_dims()
+
+    with tc.tile_pool(name="const", bufs=1) as const, tc.tile_pool(
+        name="raw", bufs=6
+    ) as raw_pool, tc.tile_pool(name="stage", bufs=4) as stage, tc.tile_pool(
+        name="keep", bufs=6
+    ) as keep, tc.tile_pool(name="result", bufs=1) as result, tc.psum_pool(
+        name="flipped", bufs=4
+    ) as flipped, tc.psum_pool(name="sums", bufs=4) as sums, tc.manual_schedule():
+
+        def load_chunk(rows):
+            raw = raw_pool.tile([P, QUAD * I], BF16)
+            nc.sync.dma_start(out=raw[:].rearrange("p (g k) -> p g k", g=QUAD), in_=rows)
+            return raw
+
+        def x_chunk(q):
+            return x_rows[:, q * QUAD * I : (q + 1) * QUAD * I].rearrange("n (g k) -> n g k", g=QUAD)
+
+        def w_chunk(j, q):
+            return W[q * QUAD : (q + 1) * QUAD, j * P : (j + 1) * P, :].rearrange("g h k -> h g k")
+
+        b_rows = const.tile([P, P], BF16)
+        nc.gpsimd.memset(b_rows[:], 0.0)
+        nc.sync.dma_start(out=b_rows[0:B_ROWS, :], in_=b.rearrange("g (j h) -> (g j) h", h=P))
+        x0_raw = load_chunk(x_chunk(0))
+        w00_raw = load_chunk(w_chunk(0, 0))
+        x1_raw = load_chunk(x_chunk(1))
+        w01_raw = load_chunk(w_chunk(0, 1))
+        w10_raw = load_chunk(w_chunk(1, 0))
+        w11_raw = load_chunk(w_chunk(1, 1))
+
+        ident_bf = const.tile([P, P], BF16)
+        make_identity(nc, ident_bf[:])
+        ident = const.tile([P, P], F32)
+        make_identity(nc, ident[:])
+
+        def transpose_and_quantise(raw):
+            codes = keep.tile([P, QUAD * P], U32, align_bytes=64)
+            scales = keep.tile([P, QUAD * P], U8, align_bytes=64)
+            words = raw[:].bitcast(F32)
+            for pair in range(QUAD // 2):
+                bank = flipped.tile([P, 2, 2, P], F32, tag="bank")
+                for g in range(2):
+                    for u in range(2):
+                        first = (2 * pair + g) * 2 * P
+                        nc.tensor.transpose(
+                            bank[:, g, u, :], words[:, first + u : first + 2 * P : 2], ident[:]
+                        )
+                grouped = stage.tile([P, 2 * P * 4], BF16, align_bytes=64)
+                nc.scalar.copy(
+                    out=grouped[:].bitcast(F32).rearrange("p (g r u) -> p g r u", g=2, u=2),
+                    in_=bank[:].rearrange("p g u r -> p g r u"),
+                )
+                cols = slice(pair * 2 * P, (pair + 1) * 2 * P)
+                nc.vector.quantize_mx(
+                    out=codes[:, cols].bitcast(FP8X4), scales=scales[:, cols], in_=grouped[:]
+                )
+            return codes, scales
+
+        def spread_bias():
+            b_flipped = flipped.tile([P, P], BF16, tag="bank")
+            nc.tensor.transpose(b_flipped[:], b_rows[:], ident_bf[:])
+            b_cols = const.tile([P, B_ROWS], BF16)
+            nc.vector.tensor_copy(out=b_cols[:], in_=b_flipped[:, 0:B_ROWS])
+            bias = const.tile([P, G * H], BF16)
+            for half in range(2):
+                spread = flipped.tile([P, B_ROWS // 2, P], BF16, tag="bank")
+                for k in range(B_ROWS // 2):
+                    c = half * (B_ROWS // 2) + k
+                    nc.tensor.transpose(
+                        spread[:, k, :], b_cols[:, c : c + 1].to_broadcast([P, P]), ident_bf[:]
+                    )
+                nc.vector.tensor_copy(
+                    out=bias[:, half * G * P : (half + 1) * G * P],
+                    in_=spread[:].rearrange("p k n -> p (k n)"),
+                )
+            return bias[:].rearrange("p (g h) -> p g h", g=G)
+
+        def multiply(x_mx, w_mx, shuffled, j, q):
+            x_codes, x_scales = x_mx
+            w_codes, w_scales = w_mx
+            acc = sums.tile([P, QUAD, P], F32)
+            for g in range(QUAD):
+                cols = slice(g * P, (g + 1) * P)
+                nc.tensor.matmul_mx(
+                    out=acc[:, g, :],
+                    lhsT=x_codes[:, cols].bitcast(FP8X4),
+                    lhsT_scale=x_scales[:, cols],
+                    rhs=w_codes[:, cols].bitcast(FP8X4),
+                    rhs_scale=w_scales[:, cols],
+                    start=True,
+                    stop=True,
+                )
+            groups = slice(q * QUAD, (q + 1) * QUAD)
+            nc.vector.tensor_tensor(
+                out=shuffled[:, :, groups],
+                in0=acc[:].rearrange("p g h -> p h g"),
+                in1=bias_gh[:, groups, j * P : (j + 1) * P].rearrange("p g h -> p h g"),
+                op=mybir.AluOpType.add,
+            )
+
+        def store(shuffled, j):
+            nc.sync.dma_start(
+                out=out_rows[:, j * P * G : (j + 1) * P * G],
+                in_=shuffled[:].rearrange("p h g -> p (h g)"),
+            )
+
+        first_half = result.tile([P, P, G], F32)
+        second_half = result.tile([P, P, G], F32)
+        bias_gh = spread_bias()
+        x0 = transpose_and_quantise(x0_raw)
+        w00 = transpose_and_quantise(w00_raw)
+        x1 = transpose_and_quantise(x1_raw)
+        multiply(x0, w00, first_half, 0, 0)
+        w01 = transpose_and_quantise(w01_raw)
+        w10 = transpose_and_quantise(w10_raw)
+        multiply(x1, w01, first_half, 0, 1)
+        store(first_half, 0)
+        w11 = transpose_and_quantise(w11_raw)
+        multiply(x0, w10, second_half, 1, 0)
+        multiply(x1, w11, second_half, 1, 1)
+        store(second_half, 1)

@@ -12,7 +12,6 @@ G = 8
 I = 512
 H = 256
 QUAD = 4
-B_ROWS = G * H // P
 
 FLOPS = 2 * P * G * I * H
 
@@ -41,9 +40,9 @@ def tile_groupedlinear_s_kernel(tc, x, W, b, out):
         def w_chunk(j, q):
             return W[q * QUAD : (q + 1) * QUAD, j * P : (j + 1) * P, :].rearrange("g h k -> h g k")
 
-        b_rows = const.tile([P, P], BF16)
+        b_rows = const.tile([P, P], F32)
         nc.gpsimd.memset(b_rows[:], 0.0)
-        nc.sync.dma_start(out=b_rows[0:B_ROWS, :], in_=b.rearrange("g (j h) -> (g j) h", h=P))
+        nc.sync.dma_start(out=b_rows[0:G, :], in_=b.bitcast(F32))
         x0_raw = load_chunk(x_chunk(0))
         w00_raw = load_chunk(w_chunk(0, 0))
         x1_raw = load_chunk(x_chunk(1))
@@ -51,8 +50,6 @@ def tile_groupedlinear_s_kernel(tc, x, W, b, out):
         w10_raw = load_chunk(w_chunk(1, 0))
         w11_raw = load_chunk(w_chunk(1, 1))
 
-        ident_bf = const.tile([P, P], BF16)
-        make_identity(nc, ident_bf[:])
         ident = const.tile([P, P], F32)
         make_identity(nc, ident[:])
 
@@ -80,20 +77,20 @@ def tile_groupedlinear_s_kernel(tc, x, W, b, out):
             return codes, scales
 
         def spread_bias():
-            b_flipped = flipped.tile([P, P], BF16, tag="bank")
-            nc.tensor.transpose(b_flipped[:], b_rows[:], ident_bf[:])
-            b_cols = const.tile([P, B_ROWS], BF16)
-            nc.vector.tensor_copy(out=b_cols[:], in_=b_flipped[:, 0:B_ROWS])
+            b_flipped = flipped.tile([P, P], F32, tag="bank")
+            nc.tensor.transpose(b_flipped[:], b_rows[:], ident[:])
+            b_cols = const.tile([P, G], F32)
+            nc.vector.tensor_copy(out=b_cols[:], in_=b_flipped[:, 0:G])
             bias = const.tile([P, G * H], BF16)
             for half in range(2):
-                spread = flipped.tile([P, B_ROWS // 2, P], BF16, tag="bank")
-                for k in range(B_ROWS // 2):
-                    c = half * (B_ROWS // 2) + k
+                spread = flipped.tile([P, QUAD, P], F32, tag="bank")
+                for k in range(QUAD):
+                    g = half * QUAD + k
                     nc.tensor.transpose(
-                        spread[:, k, :], b_cols[:, c : c + 1].to_broadcast([P, P]), ident_bf[:]
+                        spread[:, k, :], b_cols[:, g : g + 1].to_broadcast([P, P]), ident[:]
                     )
                 nc.vector.tensor_copy(
-                    out=bias[:, half * G * P : (half + 1) * G * P],
+                    out=bias[:].bitcast(F32)[:, half * QUAD * P : (half + 1) * QUAD * P],
                     in_=spread[:].rearrange("p k n -> p (k n)"),
                 )
             return bias[:].rearrange("p (g h) -> p g h", g=G)

@@ -30,7 +30,7 @@ def tile_groupedlinear_s_kernel(tc, x, W, b, out):
     ) as flipped, tc.psum_pool(name="sums", bufs=4) as sums, tc.manual_schedule():
 
         def load_chunk(rows):
-            raw = raw_pool.tile([P, QUAD * I], BF16)
+            raw = raw_pool.tile([P, QUAD * I], BF16, tag="raw")
             nc.sync.dma_start(out=raw[:].rearrange("p (g k) -> p g k", g=QUAD), in_=rows)
             return raw
 
@@ -43,7 +43,10 @@ def tile_groupedlinear_s_kernel(tc, x, W, b, out):
         b_rows = const.tile([P, P], F32)
         nc.gpsimd.memset(b_rows[:], 0.0)
         nc.sync.dma_start(out=b_rows[0:G, :], in_=b.bitcast(F32))
-        x0_raw = load_chunk(x_chunk(0))
+        x0_raw = raw_pool.tile([P, QUAD * I], BF16, tag="raw")
+        for half in range(2):
+            cols = slice(half * 2 * I, (half + 1) * 2 * I)
+            nc.sync.dma_start(out=x0_raw[:, cols], in_=x_rows[:, cols])
         w00_raw = load_chunk(w_chunk(0, 0))
         x1_raw = load_chunk(x_chunk(1))
         w01_raw = load_chunk(w_chunk(0, 1))
@@ -53,7 +56,7 @@ def tile_groupedlinear_s_kernel(tc, x, W, b, out):
         ident = const.tile([P, P], F32)
         make_identity(nc, ident[:])
 
-        def transpose_and_quantise(raw):
+        def transpose_and_quantise(raw, after_pair=lambda pair: None):
             codes = keep.tile([P, QUAD * P], U32, align_bytes=64)
             scales = keep.tile([P, QUAD * P], U8, align_bytes=64)
             words = raw[:].bitcast(F32)
@@ -74,28 +77,32 @@ def tile_groupedlinear_s_kernel(tc, x, W, b, out):
                 nc.vector.quantize_mx(
                     out=codes[:, cols].bitcast(FP8X4), scales=scales[:, cols], in_=grouped[:]
                 )
+                after_pair(pair)
             return codes, scales
 
-        def spread_bias():
+        bias = const.tile([P, G * H], BF16)
+        bias_gh = bias[:].rearrange("p (g h) -> p g h", g=G)
+
+        def flip_bias():
             b_flipped = flipped.tile([P, P], F32, tag="bank")
             nc.tensor.transpose(b_flipped[:], b_rows[:], ident[:])
             b_cols = const.tile([P, G], F32)
             nc.vector.tensor_copy(out=b_cols[:], in_=b_flipped[:, 0:G])
-            bias = const.tile([P, G * H], BF16)
-            for half in range(2):
-                spread = flipped.tile([P, QUAD, P], F32, tag="bank")
-                for k in range(QUAD):
-                    g = half * QUAD + k
-                    nc.tensor.transpose(
-                        spread[:, k, :], b_cols[:, g : g + 1].to_broadcast([P, P]), ident[:]
-                    )
-                nc.vector.tensor_copy(
-                    out=bias[:].bitcast(F32)[:, half * QUAD * P : (half + 1) * QUAD * P],
-                    in_=spread[:].rearrange("p k n -> p (k n)"),
-                )
-            return bias[:].rearrange("p (g h) -> p g h", g=G)
+            return b_cols
 
-        def multiply(x_mx, w_mx, shuffled, j, q):
+        def spread_bias(half):
+            spread = flipped.tile([P, QUAD, P], F32, tag="bank")
+            for k in range(QUAD):
+                g = half * QUAD + k
+                nc.tensor.transpose(
+                    spread[:, k, :], b_cols[:, g : g + 1].to_broadcast([P, P]), ident[:]
+                )
+            nc.vector.tensor_copy(
+                out=bias[:].bitcast(F32)[:, half * QUAD * P : (half + 1) * QUAD * P],
+                in_=spread[:].rearrange("p k n -> p (k n)"),
+            )
+
+        def multiply(x_mx, w_mx, shuffled, j, q, parts=(slice(0, P),), then=lambda part: None):
             x_codes, x_scales = x_mx
             w_codes, w_scales = w_mx
             acc = sums.tile([P, QUAD, P], F32)
@@ -111,23 +118,25 @@ def tile_groupedlinear_s_kernel(tc, x, W, b, out):
                     stop=True,
                 )
             groups = slice(q * QUAD, (q + 1) * QUAD)
-            nc.vector.tensor_tensor(
-                out=shuffled[:, :, groups],
-                in0=acc[:].rearrange("p g h -> p h g"),
-                in1=bias_gh[:, groups, j * P : (j + 1) * P].rearrange("p g h -> p h g"),
-                op=mybir.AluOpType.add,
-            )
+            for part in parts:
+                nc.vector.tensor_tensor(
+                    out=shuffled[:, part, groups],
+                    in0=acc[:, :, part].rearrange("p g h -> p h g"),
+                    in1=bias_gh[:, groups, j * P + part.start : j * P + part.stop].rearrange("p g h -> p h g"),
+                    op=mybir.AluOpType.add,
+                )
+                then(part)
 
-        def store(shuffled, j):
+        def store(shuffled, j, part=slice(0, P)):
             nc.sync.dma_start(
-                out=out_rows[:, j * P * G : (j + 1) * P * G],
-                in_=shuffled[:].rearrange("p h g -> p (h g)"),
+                out=out_rows[:, (j * P + part.start) * G : (j * P + part.stop) * G],
+                in_=shuffled[:, part, :].rearrange("p h g -> p (h g)"),
             )
 
         first_half = result.tile([P, P, G], F32)
         second_half = result.tile([P, P, G], F32)
-        bias_gh = spread_bias()
-        x0 = transpose_and_quantise(x0_raw)
+        b_cols = flip_bias()
+        x0 = transpose_and_quantise(x0_raw, spread_bias)
         w00 = transpose_and_quantise(w00_raw)
         x1 = transpose_and_quantise(x1_raw)
         multiply(x0, w00, first_half, 0, 0)
@@ -137,5 +146,8 @@ def tile_groupedlinear_s_kernel(tc, x, W, b, out):
         store(first_half, 0)
         w11 = transpose_and_quantise(w11_raw)
         multiply(x0, w10, second_half, 1, 0)
-        multiply(x1, w11, second_half, 1, 1)
-        store(second_half, 1)
+        multiply(
+            x1, w11, second_half, 1, 1,
+            parts=(slice(0, P // 2), slice(P // 2, P)),
+            then=lambda part: store(second_half, 1, part),
+        )

@@ -12,6 +12,7 @@ G = 8
 I = 512
 H = 256
 QUAD = 4
+Q = 32
 
 FLOPS = 2 * P * G * I * H
 
@@ -40,13 +41,15 @@ def tile_groupedlinear_s_kernel(tc, x, W, b, out):
         def w_chunk(j, q):
             return W[q * QUAD : (q + 1) * QUAD, j * P : (j + 1) * P, :].rearrange("g h k -> h g k")
 
-        b_rows = const.tile([P, P], F32)
-        nc.gpsimd.memset(b_rows[:], 0.0)
-        nc.sync.dma_start(out=b_rows[0:G, :], in_=b.bitcast(F32))
         x0_raw = raw_pool.tile([P, QUAD * I], BF16, tag="raw")
-        for half in range(2):
-            cols = slice(half * 2 * I, (half + 1) * 2 * I)
-            nc.sync.dma_start(out=x0_raw[:, cols], in_=x_rows[:, cols])
+        nc.sync.dma_start(out=x0_raw[:, 0 : 2 * I], in_=x_rows[:, 0 : 2 * I])
+        b_rows = const.tile([P, Q], F32, align_bytes=64)
+        for first in range(0, P, Q):
+            nc.sync.dma_start(
+                out=b_rows[first : first + Q, :],
+                in_=b.bitcast(F32).rearrange("g (q i) -> (g q) i", i=Q),
+            )
+        nc.sync.dma_start(out=x0_raw[:, 2 * I : 4 * I], in_=x_rows[:, 2 * I : 4 * I])
         w00_raw = load_chunk(w_chunk(0, 0))
         x1_raw = load_chunk(x_chunk(1))
         w01_raw = load_chunk(w_chunk(0, 1))
@@ -56,7 +59,7 @@ def tile_groupedlinear_s_kernel(tc, x, W, b, out):
         ident = const.tile([P, P], F32)
         make_identity(nc, ident[:])
 
-        def transpose_and_quantise(raw, after_pair=lambda pair: None):
+        def transpose_and_quantise(raw):
             codes = keep.tile([P, QUAD * P], U32, align_bytes=64)
             scales = keep.tile([P, QUAD * P], U8, align_bytes=64)
             words = raw[:].bitcast(F32)
@@ -77,29 +80,25 @@ def tile_groupedlinear_s_kernel(tc, x, W, b, out):
                 nc.vector.quantize_mx(
                     out=codes[:, cols].bitcast(FP8X4), scales=scales[:, cols], in_=grouped[:]
                 )
-                after_pair(pair)
             return codes, scales
 
-        bias = const.tile([P, G * H], BF16)
-        bias_gh = bias[:].rearrange("p (g h) -> p g h", g=G)
+        bias = const.tile([P, Q * Q], F32, align_bytes=64)
+        bias_gh = bias[:].bitcast(BF16).rearrange("p (g h) -> p g h", g=G)
 
-        def flip_bias():
-            b_flipped = flipped.tile([P, P], F32, tag="bank")
-            nc.tensor.transpose(b_flipped[:], b_rows[:], ident[:])
-            b_cols = const.tile([P, G], F32)
-            nc.vector.tensor_copy(out=b_cols[:], in_=b_flipped[:, 0:G])
-            return b_cols
+        def repeat_bias():
+            b_cols = const.tile([P, Q], F32, align_bytes=64)
+            nc.vector.transpose(out=b_cols[:], in_=b_rows[:])
+            repeated = const.tile([P, Q, Q], F32, align_bytes=64)
+            nc.vector.tensor_copy(
+                out=repeated[:], in_=b_cols[:].unsqueeze(2).to_broadcast([P, Q, Q])
+            )
+            return repeated
 
         def spread_bias(half):
-            spread = flipped.tile([P, QUAD, P], F32, tag="bank")
-            for k in range(QUAD):
-                g = half * QUAD + k
-                nc.tensor.transpose(
-                    spread[:, k, :], b_cols[:, g : g + 1].to_broadcast([P, P]), ident[:]
-                )
-            nc.vector.tensor_copy(
-                out=bias[:].bitcast(F32)[:, half * QUAD * P : (half + 1) * QUAD * P],
-                in_=spread[:].rearrange("p k n -> p (k n)"),
+            blocks = slice(half * Q // 2, (half + 1) * Q // 2)
+            words = slice(half * Q * Q // 2, (half + 1) * Q * Q // 2)
+            nc.vector.transpose(
+                out=bias[:, words], in_=repeated[:, blocks, :].rearrange("p b i -> p (b i)")
             )
 
         def multiply(x_mx, w_mx, shuffled, j, q, parts=(slice(0, P),), then=lambda part: None):
@@ -135,8 +134,10 @@ def tile_groupedlinear_s_kernel(tc, x, W, b, out):
 
         first_half = result.tile([P, P, G], F32)
         second_half = result.tile([P, P, G], F32)
-        b_cols = flip_bias()
-        x0 = transpose_and_quantise(x0_raw, spread_bias)
+        repeated = repeat_bias()
+        spread_bias(0)
+        x0 = transpose_and_quantise(x0_raw)
+        spread_bias(1)
         w00 = transpose_and_quantise(w00_raw)
         x1 = transpose_and_quantise(x1_raw)
         multiply(x0, w00, first_half, 0, 0)

@@ -25,7 +25,7 @@ def tile_groupedlinear_s_kernel(tc, x, W, b, out):
     with tc.tile_pool(name="const", bufs=1) as const, tc.tile_pool(
         name="raw", bufs=6
     ) as raw_pool, tc.tile_pool(name="stage", bufs=4) as stage, tc.tile_pool(
-        name="keep", bufs=6
+        name="keep", bufs=12
     ) as keep, tc.tile_pool(name="result", bufs=1) as result, tc.psum_pool(
         name="flipped", bufs=4
     ) as flipped, tc.psum_pool(name="sums", bufs=4) as sums, tc.manual_schedule():
@@ -42,45 +42,59 @@ def tile_groupedlinear_s_kernel(tc, x, W, b, out):
             return W[q * QUAD : (q + 1) * QUAD, j * P : (j + 1) * P, :].rearrange("g h k -> h g k")
 
         x0_raw = raw_pool.tile([P, QUAD * I], BF16, tag="raw")
-        nc.sync.dma_start(out=x0_raw[:, 0 : 2 * I], in_=x_rows[:, 0 : 2 * I])
+        nc.sync.dma_start(out=x0_raw[:, 0 : 1024], in_=x_rows[:, 0 : 1024])
         b_rows = const.tile([P, Q], F32, align_bytes=64)
         for first in range(0, P, Q):
             nc.sync.dma_start(
                 out=b_rows[first : first + Q, :],
                 in_=b.bitcast(F32).rearrange("g (q i) -> (g q) i", i=Q),
             )
-        nc.sync.dma_start(out=x0_raw[:, 2 * I : 4 * I], in_=x_rows[:, 2 * I : 4 * I])
-        w00_raw = load_chunk(w_chunk(0, 0))
-        x1_raw = load_chunk(x_chunk(1))
-        w01_raw = load_chunk(w_chunk(0, 1))
-        w10_raw = load_chunk(w_chunk(1, 0))
-        w11_raw = load_chunk(w_chunk(1, 1))
-
+        nc.sync.dma_start(out=x0_raw[:, 1024 : 2048], in_=x_rows[:, 1024 : 2048])
+        w00_raw = raw_pool.tile([P, QUAD * I], BF16, tag="raw")
+        nc.sync.dma_start(out=w00_raw[:, 0 : 1024].rearrange("p (g k) -> p g k", g=2), in_=W[0 : 2, 0 : 128, :].rearrange("g h k -> h g k"))
+        nc.sync.dma_start(out=w00_raw[:, 1024 : 2048].rearrange("p (g k) -> p g k", g=2), in_=W[2 : 4, 0 : 128, :].rearrange("g h k -> h g k"))
+        x1_raw = raw_pool.tile([P, QUAD * I], BF16, tag="raw")
+        nc.sync.dma_start(out=x1_raw[:, 0 : 1024], in_=x_rows[:, 2048 : 3072])
+        nc.sync.dma_start(out=x1_raw[:, 1024 : 2048], in_=x_rows[:, 3072 : 4096])
+        w01_raw = raw_pool.tile([P, QUAD * I], BF16, tag="raw")
+        nc.sync.dma_start(out=w01_raw[:, 0 : 1024].rearrange("p (g k) -> p g k", g=2), in_=W[4 : 6, 0 : 128, :].rearrange("g h k -> h g k"))
+        nc.sync.dma_start(out=w01_raw[:, 1024 : 2048].rearrange("p (g k) -> p g k", g=2), in_=W[6 : 8, 0 : 128, :].rearrange("g h k -> h g k"))
+        w10_raw = raw_pool.tile([P, QUAD * I], BF16, tag="raw")
+        nc.sync.dma_start(out=w10_raw[:, 0 : 1024].rearrange("p (g k) -> p g k", g=2), in_=W[0 : 2, 128 : 256, :].rearrange("g h k -> h g k"))
+        nc.sync.dma_start(out=w10_raw[:, 1024 : 2048].rearrange("p (g k) -> p g k", g=2), in_=W[2 : 4, 128 : 256, :].rearrange("g h k -> h g k"))
+        w11_raw = raw_pool.tile([P, QUAD * I], BF16, tag="raw")
+        nc.sync.dma_start(out=w11_raw[:, 0 : 1024].rearrange("p (g k) -> p g k", g=2), in_=W[4 : 6, 128 : 256, :].rearrange("g h k -> h g k"))
+        nc.sync.dma_start(out=w11_raw[:, 1024 : 2048].rearrange("p (g k) -> p g k", g=2), in_=W[6 : 8, 128 : 256, :].rearrange("g h k -> h g k"))
         ident = const.tile([P, P], F32)
         make_identity(nc, ident[:])
 
-        def transpose_and_quantise(raw):
-            codes = keep.tile([P, QUAD * P], U32, align_bytes=64)
-            scales = keep.tile([P, QUAD * P], U8, align_bytes=64)
+        def flip(raw, pair):
+            bank = flipped.tile([P, 2, 2, P], F32, tag="bank")
             words = raw[:].bitcast(F32)
-            for pair in range(QUAD // 2):
-                bank = flipped.tile([P, 2, 2, P], F32, tag="bank")
-                for g in range(2):
-                    for u in range(2):
-                        first = (2 * pair + g) * 2 * P
-                        nc.tensor.transpose(
-                            bank[:, g, u, :], words[:, first + u : first + 2 * P : 2], ident[:]
-                        )
-                grouped = stage.tile([P, 2 * P * 4], BF16, align_bytes=64)
-                nc.scalar.copy(
-                    out=grouped[:].bitcast(F32).rearrange("p (g r u) -> p g r u", g=2, u=2),
-                    in_=bank[:].rearrange("p g u r -> p g r u"),
-                )
-                cols = slice(pair * 2 * P, (pair + 1) * 2 * P)
-                nc.vector.quantize_mx(
-                    out=codes[:, cols].bitcast(FP8X4), scales=scales[:, cols], in_=grouped[:]
-                )
+            for g in range(2):
+                for u in range(2):
+                    first = (2 * pair + g) * 2 * P
+                    nc.tensor.transpose(
+                        bank[:, g, u, :], words[:, first + u : first + 2 * P : 2], ident[:]
+                    )
+            return bank
+
+        def gather(bank):
+            grouped = stage.tile([P, 2 * P * 4], BF16, align_bytes=64, tag="grouped")
+            nc.scalar.copy(
+                out=grouped[:].bitcast(F32).rearrange("p (g r u) -> p g r u", g=2, u=2),
+                in_=bank[:].rearrange("p g u r -> p g r u"),
+            )
+            return grouped
+
+        def quantise(grouped):
+            codes = keep.tile([P, 2 * P], U32, align_bytes=64, tag="codes")
+            scales = keep.tile([P, 2 * P], U8, align_bytes=64, tag="scales")
+            nc.vector.quantize_mx(out=codes[:].bitcast(FP8X4), scales=scales[:], in_=grouped[:])
             return codes, scales
+
+        def unit(raw, pair):
+            return quantise(gather(flip(raw, pair)))
 
         bias = const.tile([P, Q * Q], F32, align_bytes=64)
         bias_gh = bias[:].bitcast(BF16).rearrange("p (g h) -> p g h", g=G)
@@ -101,12 +115,11 @@ def tile_groupedlinear_s_kernel(tc, x, W, b, out):
                 out=bias[:, words], in_=repeated[:, blocks, :].rearrange("p b i -> p (b i)")
             )
 
-        def multiply(x_mx, w_mx, shuffled, j, q, parts=(slice(0, P),), then=lambda part: None):
-            x_codes, x_scales = x_mx
-            w_codes, w_scales = w_mx
-            acc = sums.tile([P, QUAD, P], F32)
+        def multiply(x_pairs, w_pairs):
+            acc = sums.tile([P, QUAD, P], F32, tag="acc")
             for g in range(QUAD):
-                cols = slice(g * P, (g + 1) * P)
+                (x_codes, x_scales), (w_codes, w_scales) = x_pairs[g // 2], w_pairs[g // 2]
+                cols = slice(g % 2 * P, (g % 2 + 1) * P)
                 nc.tensor.matmul_mx(
                     out=acc[:, g, :],
                     lhsT=x_codes[:, cols].bitcast(FP8X4),
@@ -116,39 +129,62 @@ def tile_groupedlinear_s_kernel(tc, x, W, b, out):
                     start=True,
                     stop=True,
                 )
-            groups = slice(q * QUAD, (q + 1) * QUAD)
-            for part in parts:
-                nc.vector.tensor_tensor(
-                    out=shuffled[:, part, groups],
-                    in0=acc[:, :, part].rearrange("p g h -> p h g"),
-                    in1=bias_gh[:, groups, j * P + part.start : j * P + part.stop].rearrange("p g h -> p h g"),
-                    op=mybir.AluOpType.add,
-                )
-                then(part)
+            return acc
 
-        def store(shuffled, j, part=slice(0, P)):
+        def add_bias(acc, j, q, part=slice(0, P)):
+            groups = slice(q * QUAD, (q + 1) * QUAD)
+            nc.vector.tensor_tensor(
+                out=shuffled[j][:, part, groups],
+                in0=acc[:, :, part].rearrange("p g h -> p h g"),
+                in1=bias_gh[:, groups, j * P + part.start : j * P + part.stop].rearrange("p g h -> p h g"),
+                op=mybir.AluOpType.add,
+            )
+
+        def store(j, part=slice(0, P)):
             nc.sync.dma_start(
                 out=out_rows[:, (j * P + part.start) * G : (j * P + part.stop) * G],
-                in_=shuffled[:, part, :].rearrange("p h g -> p (h g)"),
+                in_=shuffled[j][:, part, :].rearrange("p h g -> p (h g)"),
             )
 
         first_half = result.tile([P, P, G], F32)
         second_half = result.tile([P, P, G], F32)
+        shuffled = (first_half, second_half)
+        mx = {}
         repeated = repeat_bias()
         spread_bias(0)
-        x0 = transpose_and_quantise(x0_raw)
+        bank = flip(x0_raw, 0)
+        mx["x0_0"] = quantise(gather(bank))
         spread_bias(1)
-        w00 = transpose_and_quantise(w00_raw)
-        x1 = transpose_and_quantise(x1_raw)
-        multiply(x0, w00, first_half, 0, 0)
-        w01 = transpose_and_quantise(w01_raw)
-        w10 = transpose_and_quantise(w10_raw)
-        multiply(x1, w01, first_half, 0, 1)
-        store(first_half, 0)
-        w11 = transpose_and_quantise(w11_raw)
-        multiply(x0, w10, second_half, 1, 0)
-        multiply(
-            x1, w11, second_half, 1, 1,
-            parts=(slice(0, P // 2), slice(P // 2, P)),
-            then=lambda part: store(second_half, 1, part),
-        )
+        bank = flip(x0_raw, 1)
+        mx["x0_1"] = quantise(gather(bank))
+        bank = flip(w00_raw, 0)
+        mx["w00_0"] = quantise(gather(bank))
+        bank = flip(w00_raw, 1)
+        mx["w00_1"] = quantise(gather(bank))
+        bank = flip(x1_raw, 0)
+        mx["x1_0"] = quantise(gather(bank))
+        bank = flip(x1_raw, 1)
+        acc_a = multiply([mx["x0_0"], mx["x0_1"]], [mx["w00_0"], mx["w00_1"]])
+        add_bias(acc_a, 0, 0)
+        mx["x1_1"] = quantise(gather(bank))
+        bank = flip(w01_raw, 0)
+        mx["w01_0"] = quantise(gather(bank))
+        bank = flip(w01_raw, 1)
+        mx["w01_1"] = quantise(gather(bank))
+        bank = flip(w10_raw, 0)
+        mx["w10_0"] = quantise(gather(bank))
+        bank = flip(w10_raw, 1)
+        acc_b = multiply([mx["x1_0"], mx["x1_1"]], [mx["w01_0"], mx["w01_1"]])
+        add_bias(acc_b, 0, 1)
+        store(0)
+        mx["w10_1"] = quantise(gather(bank))
+        bank = flip(w11_raw, 0)
+        mx["w11_0"] = quantise(gather(bank))
+        bank = flip(w11_raw, 1)
+        mx["w11_1"] = quantise(gather(bank))
+        acc_c = multiply([mx["x0_0"], mx["x0_1"]], [mx["w10_0"], mx["w10_1"]])
+        add_bias(acc_c, 1, 0)
+        acc_d = multiply([mx["x1_0"], mx["x1_1"]], [mx["w11_0"], mx["w11_1"]])
+        for part in (slice(0, P // 2), slice(P // 2, P)):
+            add_bias(acc_d, 1, 1, part)
+            store(1, part)

@@ -23,7 +23,7 @@ def tile_groupedlinear_s_kernel(tc, x, W, b, out):
     out_rows = out.flatten_outer_dims()
 
     with tc.tile_pool(name="const", bufs=1) as const, tc.tile_pool(
-        name="raw", bufs=6
+        name="raw", bufs=12
     ) as raw_pool, tc.tile_pool(name="stage", bufs=4) as stage, tc.tile_pool(
         name="keep", bufs=12
     ) as keep, tc.tile_pool(name="result", bufs=1) as result, tc.psum_pool(
@@ -41,60 +41,58 @@ def tile_groupedlinear_s_kernel(tc, x, W, b, out):
         def w_chunk(j, q):
             return W[q * QUAD : (q + 1) * QUAD, j * P : (j + 1) * P, :].rearrange("g h k -> h g k")
 
-        x0_raw = raw_pool.tile([P, QUAD * I], BF16, tag="raw")
-        nc.sync.dma_start(out=x0_raw[:, 0 : 1024], in_=x_rows[:, 0 : 1024])
+        def load(n, rows):
+            raw = raw_pool.tile([P, n * I], BF16, tag=f"raw{n}")
+            nc.sync.dma_start(out=raw[:].rearrange("p (g k) -> p g k", g=n), in_=rows)
+            return raw
+
+        raw_x0_0 = load(2, x_rows[:, 0 : 1024].rearrange("n (g k) -> n g k", g=2))
         b_rows = const.tile([P, Q], F32, align_bytes=64)
         for first in range(0, P, Q):
             nc.sync.dma_start(
                 out=b_rows[first : first + Q, :],
                 in_=b.bitcast(F32).rearrange("g (q i) -> (g q) i", i=Q),
             )
-        nc.sync.dma_start(out=x0_raw[:, 1024 : 2048], in_=x_rows[:, 1024 : 2048])
-        w00_raw = raw_pool.tile([P, QUAD * I], BF16, tag="raw")
-        nc.sync.dma_start(out=w00_raw[:, 0 : 1024].rearrange("p (g k) -> p g k", g=2), in_=W[0 : 2, 0 : 128, :].rearrange("g h k -> h g k"))
-        nc.sync.dma_start(out=w00_raw[:, 1024 : 2048].rearrange("p (g k) -> p g k", g=2), in_=W[2 : 4, 0 : 128, :].rearrange("g h k -> h g k"))
-        x1_raw = raw_pool.tile([P, QUAD * I], BF16, tag="raw")
-        nc.sync.dma_start(out=x1_raw[:, 0 : 1024], in_=x_rows[:, 2048 : 3072])
-        nc.sync.dma_start(out=x1_raw[:, 1024 : 2048], in_=x_rows[:, 3072 : 4096])
-        w01_raw = raw_pool.tile([P, QUAD * I], BF16, tag="raw")
-        nc.sync.dma_start(out=w01_raw[:, 0 : 1024].rearrange("p (g k) -> p g k", g=2), in_=W[4 : 6, 0 : 128, :].rearrange("g h k -> h g k"))
-        nc.sync.dma_start(out=w01_raw[:, 1024 : 2048].rearrange("p (g k) -> p g k", g=2), in_=W[6 : 8, 0 : 128, :].rearrange("g h k -> h g k"))
-        w10_raw = raw_pool.tile([P, QUAD * I], BF16, tag="raw")
-        nc.sync.dma_start(out=w10_raw[:, 0 : 1024].rearrange("p (g k) -> p g k", g=2), in_=W[0 : 2, 128 : 256, :].rearrange("g h k -> h g k"))
-        nc.sync.dma_start(out=w10_raw[:, 1024 : 2048].rearrange("p (g k) -> p g k", g=2), in_=W[2 : 4, 128 : 256, :].rearrange("g h k -> h g k"))
-        w11_raw = raw_pool.tile([P, QUAD * I], BF16, tag="raw")
-        nc.sync.dma_start(out=w11_raw[:, 0 : 1024].rearrange("p (g k) -> p g k", g=2), in_=W[4 : 6, 128 : 256, :].rearrange("g h k -> h g k"))
-        nc.sync.dma_start(out=w11_raw[:, 1024 : 2048].rearrange("p (g k) -> p g k", g=2), in_=W[6 : 8, 128 : 256, :].rearrange("g h k -> h g k"))
+        raw_x0_1 = load(2, x_rows[:, 1024 : 2048].rearrange("n (g k) -> n g k", g=2))
+        raw_w00_0 = load(2, W[0 : 2, 0 : 128, :].rearrange("g h k -> h g k"))
+        raw_w00_1 = load(2, W[2 : 4, 0 : 128, :].rearrange("g h k -> h g k"))
+        raw_x1_0 = load(2, x_rows[:, 2048 : 3072].rearrange("n (g k) -> n g k", g=2))
+        raw_x1_1 = load(2, x_rows[:, 3072 : 4096].rearrange("n (g k) -> n g k", g=2))
+        raw_w01_0 = load(2, W[4 : 6, 0 : 128, :].rearrange("g h k -> h g k"))
+        raw_w01_1 = load(2, W[6 : 8, 0 : 128, :].rearrange("g h k -> h g k"))
+        raw_w10_0 = load(2, W[0 : 2, 128 : 256, :].rearrange("g h k -> h g k"))
+        raw_w10_1 = load(2, W[2 : 4, 128 : 256, :].rearrange("g h k -> h g k"))
+        raw_w11_0 = load(2, W[4 : 6, 128 : 256, :].rearrange("g h k -> h g k"))
+        raw_w11_2 = load(1, W[6 : 7, 128 : 256, :].rearrange("g h k -> h g k"))
+        raw_w11_3 = load(1, W[7 : 8, 128 : 256, :].rearrange("g h k -> h g k"))
+
         ident = const.tile([P, P], F32)
         make_identity(nc, ident[:])
 
-        def flip(raw, pair):
-            bank = flipped.tile([P, 2, 2, P], F32, tag="bank")
+        def flip(raw, n):
+            bank = flipped.tile([P, n, 2, P], F32, tag="bank")
             words = raw[:].bitcast(F32)
-            for g in range(2):
+            for g in range(n):
                 for u in range(2):
-                    first = (2 * pair + g) * 2 * P
                     nc.tensor.transpose(
-                        bank[:, g, u, :], words[:, first + u : first + 2 * P : 2], ident[:]
+                        bank[:, g, u, :], words[:, g * 2 * P + u : (g + 1) * 2 * P : 2], ident[:]
                     )
             return bank
 
-        def gather(bank):
-            grouped = stage.tile([P, 2 * P * 4], BF16, align_bytes=64, tag="grouped")
-            nc.scalar.copy(
-                out=grouped[:].bitcast(F32).rearrange("p (g r u) -> p g r u", g=2, u=2),
+        def gather(bank, n, copy):
+            grouped = stage.tile([P, n * P * 4], BF16, align_bytes=64, tag="grouped")
+            copy(
+                out=grouped[:].bitcast(F32).rearrange("p (g r u) -> p g r u", g=n, u=2),
                 in_=bank[:].rearrange("p g u r -> p g r u"),
             )
             return grouped
 
-        def quantise(grouped):
-            codes = keep.tile([P, 2 * P], U32, align_bytes=64, tag="codes")
-            scales = keep.tile([P, 2 * P], U8, align_bytes=64, tag="scales")
+        def quantise(grouped, n):
+            codes = keep.tile([P, n * P], U32, align_bytes=64, tag="codes")
+            scales = keep.tile([P, n * P], U8, align_bytes=64, tag="scales")
             nc.vector.quantize_mx(out=codes[:].bitcast(FP8X4), scales=scales[:], in_=grouped[:])
-            return codes, scales
-
-        def unit(raw, pair):
-            return quantise(gather(flip(raw, pair)))
+            blocks = [slice(g * P, (g + 1) * P) for g in range(n)]
+            return [(codes[:, cols].bitcast(FP8X4), scales[:, cols]) for cols in blocks]
 
         bias = const.tile([P, Q * Q], F32, align_bytes=64)
         bias_gh = bias[:].bitcast(BF16).rearrange("p (g h) -> p g h", g=G)
@@ -115,19 +113,12 @@ def tile_groupedlinear_s_kernel(tc, x, W, b, out):
                 out=bias[:, words], in_=repeated[:, blocks, :].rearrange("p b i -> p (b i)")
             )
 
-        def multiply(x_pairs, w_pairs):
+        def multiply(x_mx, w_mx):
             acc = sums.tile([P, QUAD, P], F32, tag="acc")
             for g in range(QUAD):
-                (x_codes, x_scales), (w_codes, w_scales) = x_pairs[g // 2], w_pairs[g // 2]
-                cols = slice(g % 2 * P, (g % 2 + 1) * P)
                 nc.tensor.matmul_mx(
-                    out=acc[:, g, :],
-                    lhsT=x_codes[:, cols].bitcast(FP8X4),
-                    lhsT_scale=x_scales[:, cols],
-                    rhs=w_codes[:, cols].bitcast(FP8X4),
-                    rhs_scale=w_scales[:, cols],
-                    start=True,
-                    stop=True,
+                    out=acc[:, g, :], lhsT=x_mx[g][0], lhsT_scale=x_mx[g][1],
+                    rhs=w_mx[g][0], rhs_scale=w_mx[g][1], start=True, stop=True,
                 )
             return acc
 
@@ -149,42 +140,57 @@ def tile_groupedlinear_s_kernel(tc, x, W, b, out):
         first_half = result.tile([P, P, G], F32)
         second_half = result.tile([P, P, G], F32)
         shuffled = (first_half, second_half)
-        mx = {}
+        mx = {"x0": [], "x1": [], "w00": [], "w01": [], "w10": [], "w11": []}
         repeated = repeat_bias()
         spread_bias(0)
-        bank = flip(x0_raw, 0)
-        mx["x0_0"] = quantise(gather(bank))
+        bank = flip(raw_x0_0, 2)
+        grouped = gather(bank, 2, nc.scalar.copy)
+        mx["x0"] += quantise(grouped, 2)
         spread_bias(1)
-        bank = flip(x0_raw, 1)
-        mx["x0_1"] = quantise(gather(bank))
-        bank = flip(w00_raw, 0)
-        mx["w00_0"] = quantise(gather(bank))
-        bank = flip(w00_raw, 1)
-        mx["w00_1"] = quantise(gather(bank))
-        bank = flip(x1_raw, 0)
-        mx["x1_0"] = quantise(gather(bank))
-        bank = flip(x1_raw, 1)
-        acc_a = multiply([mx["x0_0"], mx["x0_1"]], [mx["w00_0"], mx["w00_1"]])
+        bank = flip(raw_x0_1, 2)
+        grouped = gather(bank, 2, nc.scalar.copy)
+        mx["x0"] += quantise(grouped, 2)
+        bank = flip(raw_w00_0, 2)
+        grouped = gather(bank, 2, nc.scalar.copy)
+        mx["w00"] += quantise(grouped, 2)
+        bank = flip(raw_w00_1, 2)
+        grouped = gather(bank, 2, nc.scalar.copy)
+        mx["w00"] += quantise(grouped, 2)
+        bank = flip(raw_x1_0, 2)
+        grouped = gather(bank, 2, nc.scalar.copy)
+        mx["x1"] += quantise(grouped, 2)
+        bank = flip(raw_x1_1, 2)
+        acc_a = multiply(mx["x0"], mx["w00"])
+        grouped = gather(bank, 2, nc.scalar.copy)
         add_bias(acc_a, 0, 0)
-        mx["x1_1"] = quantise(gather(bank))
-        bank = flip(w01_raw, 0)
-        mx["w01_0"] = quantise(gather(bank))
-        bank = flip(w01_raw, 1)
-        mx["w01_1"] = quantise(gather(bank))
-        bank = flip(w10_raw, 0)
-        mx["w10_0"] = quantise(gather(bank))
-        bank = flip(w10_raw, 1)
-        acc_b = multiply([mx["x1_0"], mx["x1_1"]], [mx["w01_0"], mx["w01_1"]])
+        mx["x1"] += quantise(grouped, 2)
+        bank = flip(raw_w01_0, 2)
+        grouped = gather(bank, 2, nc.scalar.copy)
+        mx["w01"] += quantise(grouped, 2)
+        bank = flip(raw_w01_1, 2)
+        grouped = gather(bank, 2, nc.scalar.copy)
+        mx["w01"] += quantise(grouped, 2)
+        bank = flip(raw_w10_0, 2)
+        grouped = gather(bank, 2, nc.scalar.copy)
+        mx["w10"] += quantise(grouped, 2)
+        bank = flip(raw_w10_1, 2)
+        grouped = gather(bank, 2, nc.scalar.copy)
+        mx["w10"] += quantise(grouped, 2)
+        bank = flip(raw_w11_0, 2)
+        acc_b = multiply(mx["x1"], mx["w01"])
+        grouped = gather(bank, 2, nc.scalar.copy)
         add_bias(acc_b, 0, 1)
         store(0)
-        mx["w10_1"] = quantise(gather(bank))
-        bank = flip(w11_raw, 0)
-        mx["w11_0"] = quantise(gather(bank))
-        bank = flip(w11_raw, 1)
-        mx["w11_1"] = quantise(gather(bank))
-        acc_c = multiply([mx["x0_0"], mx["x0_1"]], [mx["w10_0"], mx["w10_1"]])
+        mx["w11"] += quantise(grouped, 2)
+        bank = flip(raw_w11_2, 1)
+        grouped = gather(bank, 1, nc.scalar.copy)
+        mx["w11"] += quantise(grouped, 1)
+        bank = flip(raw_w11_3, 1)
+        grouped = gather(bank, 1, nc.scalar.copy)
+        mx["w11"] += quantise(grouped, 1)
+        acc_c = multiply(mx["x0"], mx["w10"])
         add_bias(acc_c, 1, 0)
-        acc_d = multiply([mx["x1_0"], mx["x1_1"]], [mx["w11_0"], mx["w11_1"]])
-        for part in (slice(0, P // 2), slice(P // 2, P)):
+        acc_d = multiply(mx["x1"], mx["w11"])
+        for part in (slice(0, 32), slice(32, P)):
             add_bias(acc_d, 1, 1, part)
             store(1, part)

import concourse.mybir as mybir
from concourse.masks import make_identity

F32 = mybir.dt.float32
BF16 = mybir.dt.bfloat16
U32 = mybir.dt.uint32
U8 = mybir.dt.uint8
FP8X4 = mybir.dt.float8_e4m3fn_x4

P = 128
G = 8
I = 512
H = 256
QUAD = 4
Q = 32

FLOPS = 2 * P * G * I * H


def tile_groupedlinear_s_kernel(tc, x, W, b, out):
    nc = tc.nc
    x_rows = x.flatten_outer_dims()
    out_rows = out.flatten_outer_dims()

    with tc.tile_pool(name="const", bufs=1) as const, tc.tile_pool(
        name="raw", bufs=12
    ) as raw_pool, tc.tile_pool(name="stage", bufs=4) as stage, tc.tile_pool(
        name="keep", bufs=12
    ) as keep, tc.tile_pool(name="result", bufs=1) as result, tc.psum_pool(
        name="flipped", bufs=4
    ) as flipped, tc.psum_pool(name="sums", bufs=4) as sums, tc.manual_schedule():

        def load_chunk(rows):
            raw = raw_pool.tile([P, QUAD * I], BF16, tag="raw")
            nc.sync.dma_start(out=raw[:].rearrange("p (g k) -> p g k", g=QUAD), in_=rows)
            return raw

        def x_chunk(q):
            return x_rows[:, q * QUAD * I : (q + 1) * QUAD * I].rearrange("n (g k) -> n g k", g=QUAD)

        def w_chunk(j, q):
            return W[q * QUAD : (q + 1) * QUAD, j * P : (j + 1) * P, :].rearrange("g h k -> h g k")

        def load(n, rows):
            raw = raw_pool.tile([P, n * I], BF16, tag=f"raw{n}")
            nc.sync.dma_start(out=raw[:].rearrange("p (g k) -> p g k", g=n), in_=rows)
            return raw

        raw_x0_0 = load(2, x_rows[:, 0 : 1024].rearrange("n (g k) -> n g k", g=2))
        b_rows = const.tile([P, Q], F32, align_bytes=64)
        for first in range(0, P, Q):
            nc.sync.dma_start(
                out=b_rows[first : first + Q, :],
                in_=b.bitcast(F32).rearrange("g (q i) -> (g q) i", i=Q),
            )
        raw_x0_1 = load(2, x_rows[:, 1024 : 2048].rearrange("n (g k) -> n g k", g=2))
        raw_w00_0 = load(2, W[0 : 2, 0 : 128, :].rearrange("g h k -> h g k"))
        raw_w00_1 = load(2, W[2 : 4, 0 : 128, :].rearrange("g h k -> h g k"))
        raw_x1_0 = load(2, x_rows[:, 2048 : 3072].rearrange("n (g k) -> n g k", g=2))
        raw_x1_1 = load(2, x_rows[:, 3072 : 4096].rearrange("n (g k) -> n g k", g=2))
        raw_w01_0 = load(2, W[4 : 6, 0 : 128, :].rearrange("g h k -> h g k"))
        raw_w01_1 = load(2, W[6 : 8, 0 : 128, :].rearrange("g h k -> h g k"))
        raw_w10_0 = load(2, W[0 : 2, 128 : 256, :].rearrange("g h k -> h g k"))
        raw_w10_1 = load(2, W[2 : 4, 128 : 256, :].rearrange("g h k -> h g k"))
        raw_w11_0 = load(2, W[4 : 6, 128 : 256, :].rearrange("g h k -> h g k"))
        raw_w11_2 = load(1, W[6 : 7, 128 : 256, :].rearrange("g h k -> h g k"))
        raw_w11_3 = load(1, W[7 : 8, 128 : 256, :].rearrange("g h k -> h g k"))

        ident = const.tile([P, P], F32)
        make_identity(nc, ident[:])

        def flip(raw, n):
            bank = flipped.tile([P, n, 2, P], F32, tag="bank")
            words = raw[:].bitcast(F32)
            for g in range(n):
                for u in range(2):
                    nc.tensor.transpose(
                        bank[:, g, u, :], words[:, g * 2 * P + u : (g + 1) * 2 * P : 2], ident[:]
                    )
            return bank

        def gather(bank, n, copy):
            grouped = stage.tile([P, n * P * 4], BF16, align_bytes=64, tag="grouped")
            copy(
                out=grouped[:].bitcast(F32).rearrange("p (g r u) -> p g r u", g=n, u=2),
                in_=bank[:].rearrange("p g u r -> p g r u"),
            )
            return grouped

        def quantise(grouped, n):
            codes = keep.tile([P, n * P], U32, align_bytes=64, tag="codes")
            scales = keep.tile([P, n * P], U8, align_bytes=64, tag="scales")
            nc.vector.quantize_mx(out=codes[:].bitcast(FP8X4), scales=scales[:], in_=grouped[:])
            blocks = [slice(g * P, (g + 1) * P) for g in range(n)]
            return [(codes[:, cols].bitcast(FP8X4), scales[:, cols]) for cols in blocks]

        bias = const.tile([P, Q * Q], F32, align_bytes=64)
        bias_gh = bias[:].bitcast(BF16).rearrange("p (g h) -> p g h", g=G)

        def repeat_bias():
            b_cols = const.tile([P, Q], F32, align_bytes=64)
            nc.vector.transpose(out=b_cols[:], in_=b_rows[:])
            repeated = const.tile([P, Q, Q], F32, align_bytes=64)
            nc.vector.tensor_copy(
                out=repeated[:], in_=b_cols[:].unsqueeze(2).to_broadcast([P, Q, Q])
            )
            return repeated

        def spread_bias(half):
            blocks = slice(half * Q // 2, (half + 1) * Q // 2)
            words = slice(half * Q * Q // 2, (half + 1) * Q * Q // 2)
            nc.vector.transpose(
                out=bias[:, words], in_=repeated[:, blocks, :].rearrange("p b i -> p (b i)")
            )

        def multiply(x_mx, w_mx):
            acc = sums.tile([P, QUAD, P], F32, tag="acc")
            for g in range(QUAD):
                nc.tensor.matmul_mx(
                    out=acc[:, g, :], lhsT=x_mx[g][0], lhsT_scale=x_mx[g][1],
                    rhs=w_mx[g][0], rhs_scale=w_mx[g][1], start=True, stop=True,
                )
            return acc

        def add_bias(acc, j, q, part=slice(0, P)):
            groups = slice(q * QUAD, (q + 1) * QUAD)
            nc.vector.tensor_tensor(
                out=shuffled[j][:, part, groups],
                in0=acc[:, :, part].rearrange("p g h -> p h g"),
                in1=bias_gh[:, groups, j * P + part.start : j * P + part.stop].rearrange("p g h -> p h g"),
                op=mybir.AluOpType.add,
            )

        def store(j, part=slice(0, P)):
            nc.sync.dma_start(
                out=out_rows[:, (j * P + part.start) * G : (j * P + part.stop) * G],
                in_=shuffled[j][:, part, :].rearrange("p h g -> p (h g)"),
            )

        first_half = result.tile([P, P, G], F32)
        second_half = result.tile([P, P, G], F32)
        shuffled = (first_half, second_half)
        mx = {"x0": [], "x1": [], "w00": [], "w01": [], "w10": [], "w11": []}
        repeated = repeat_bias()
        spread_bias(0)
        bank = flip(raw_x0_0, 2)
        grouped = gather(bank, 2, nc.scalar.copy)
        mx["x0"] += quantise(grouped, 2)
        spread_bias(1)
        bank = flip(raw_x0_1, 2)
        grouped = gather(bank, 2, nc.scalar.copy)
        mx["x0"] += quantise(grouped, 2)
        bank = flip(raw_w00_0, 2)
        grouped = gather(bank, 2, nc.scalar.copy)
        mx["w00"] += quantise(grouped, 2)
        bank = flip(raw_w00_1, 2)
        grouped = gather(bank, 2, nc.scalar.copy)
        mx["w00"] += quantise(grouped, 2)
        bank = flip(raw_x1_0, 2)
        grouped = gather(bank, 2, nc.scalar.copy)
        mx["x1"] += quantise(grouped, 2)
        bank = flip(raw_x1_1, 2)
        acc_a = multiply(mx["x0"], mx["w00"])
        grouped = gather(bank, 2, nc.scalar.copy)
        add_bias(acc_a, 0, 0)
        mx["x1"] += quantise(grouped, 2)
        bank = flip(raw_w01_0, 2)
        grouped = gather(bank, 2, nc.scalar.copy)
        mx["w01"] += quantise(grouped, 2)
        bank = flip(raw_w01_1, 2)
        grouped = gather(bank, 2, nc.scalar.copy)
        mx["w01"] += quantise(grouped, 2)
        bank = flip(raw_w10_0, 2)
        grouped = gather(bank, 2, nc.scalar.copy)
        mx["w10"] += quantise(grouped, 2)
        bank = flip(raw_w10_1, 2)
        grouped = gather(bank, 2, nc.scalar.copy)
        mx["w10"] += quantise(grouped, 2)
        bank = flip(raw_w11_0, 2)
        acc_b = multiply(mx["x1"], mx["w01"])
        grouped = gather(bank, 2, nc.scalar.copy)
        add_bias(acc_b, 0, 1)
        store(0)
        mx["w11"] += quantise(grouped, 2)
        bank = flip(raw_w11_2, 1)
        grouped = gather(bank, 1, nc.scalar.copy)
        mx["w11"] += quantise(grouped, 1)
        bank = flip(raw_w11_3, 1)
        grouped = gather(bank, 1, nc.scalar.copy)
        mx["w11"] += quantise(grouped, 1)
        acc_c = multiply(mx["x0"], mx["w10"])
        add_bias(acc_c, 1, 0)
        acc_d = multiply(mx["x1"], mx["w11"])
        for part in (slice(0, 32), slice(32, P)):
            add_bias(acc_d, 1, 1, part)
            store(1, part)
